import numpy as np
import ml_dtypes


def mxq(x, axis, fmt="e4m3"):
    dtype, down = {"e4m3": (ml_dtypes.float8_e4m3fn, 7), "e5m2": (ml_dtypes.float8_e5m2, 14)}[fmt]
    v = np.moveaxis(np.asarray(x, np.float32).astype(ml_dtypes.bfloat16).astype(np.float64), axis, -1)
    blocks = v.reshape(v.shape[:-1] + (-1, 32))
    amax = np.abs(blocks).max(-1, keepdims=True)
    byte = np.maximum(np.where(amax > 0, np.frexp(amax)[1] - 1 + 127, 0) - down, 1)
    scale = np.exp2(byte - 127.0)
    codes = (blocks / scale).astype(np.float32).astype(dtype).astype(np.float64)
    return np.moveaxis((codes * scale).reshape(v.shape), -1, axis)


WIDE = False


def mx_kscale(k):
    if not WIDE:
        return np.ones(k)
    levels = np.array([10, -10, 5, -5, 0])
    if k % 512:
        return np.exp2(np.random.permutation(np.resize(levels, k // 32))).repeat(32)
    a = np.empty((k // 512, 16))
    for p in range(k // 512):
        a[p, :8] = np.random.permutation(np.resize(levels, 8))
        for g in range(8):
            far = levels[np.abs(levels - a[p, g]) >= 10]
            a[p, g + 8] = far[np.random.randint(len(far))]
    return np.exp2(a.ravel()).repeat(32)


BF16 = ml_dtypes.bfloat16


def bf(x):
    return np.asarray(x, np.float32).astype(BF16)


def f64(x):
    return np.asarray(x).astype(np.float64)


B, K, F, INCH, OUTCH, R = 2, 4, 128, 2048, 2048, 128


def erf(a):
    c = np.clip(a, -6.0, 6.0)
    c2 = 2.0 * c * c
    t = c.copy()
    s = c.copy()
    n = 1.0
    while np.max(np.abs(t) - 1e-18 * np.abs(s)) > 0.0:
        n += 2.0
        t = t * c2 / n
        s = s + t
    return 2.0 / np.sqrt(np.pi) * np.exp(-c * c) * s


def gelu(t):
    return 0.5 * t * (1.0 + erf(t / np.sqrt(2.0)))


def draw0():
    s = mx_kscale(INCH)
    return {
        "h": bf(gelu(np.random.standard_normal((B, K, F, INCH))) * s),
        "z": bf(np.random.standard_normal((B, K, F, R)) * 0.35),
        "u": bf(np.random.standard_normal((B, K, OUTCH, R)) * 1.5 * np.sqrt(R)),
        "b": bf(np.random.standard_normal((B, 1, 1, OUTCH)) * 0.3),
        "W_out": bf(np.random.standard_normal((OUTCH, INCH)) * 1.5 / np.sqrt(INCH) / s),
        "b_out": bf(np.random.standard_normal(OUTCH) * 0.3),
    }


def core(h, z, u, b, W_out, b_out):
    lora = f64(z) @ f64(u).transpose(0, 1, 3, 2) / R
    main = mxq(f64(h), 3, "e4m3") @ mxq(f64(W_out).T, 0, "e4m3")
    return gelu(main + f64(b_out) + lora + f64(b))


def e4m3fn_bytes(y):
    return np.clip(np.asarray(y, np.float64), -448.0, 448.0).astype(np.float32).astype(ml_dtypes.float8_e4m3fn).view(np.uint8)


def e4m3fn_values(b):
    return np.asarray(b, np.uint8).view(ml_dtypes.float8_e4m3fn).astype(np.float64)


def setup_inputs():
    d = draw0()
    x0 = np.asarray(d['W_out']).astype(np.float64)
    s = (np.max(np.abs(x0), axis=(0,), keepdims=True) / 448.0).astype(np.float32)
    out = {}
    for k, v in d.items():
        if k == 'W_out':
            out['W_out_bytes'] = e4m3fn_bytes(x0 / s.astype(np.float64))
            out['W_out_scale'] = s
        else:
            out[k] = v
    return out


def reference(h, z, u, b, W_out_bytes, W_out_scale, b_out):
    return core(h, z, u, b, e4m3fn_values(W_out_bytes) * W_out_scale.astype(np.float64), b_out)

@@ -1,0 +1,309 @@
+from contextlib import ExitStack
+
+import concourse.mybir as mybir
+from concourse.masks import make_identity
+
+F32 = mybir.dt.float32
+BF16 = mybir.dt.bfloat16
+U32 = mybir.dt.uint32
+U8 = mybir.dt.uint8
+FP8 = mybir.dt.float8_e4m3fn
+FP8X4 = mybir.dt.float8_e4m3fn_x4
+ALU = mybir.AluOpType
+ACT = mybir.ActivationFunctionType
+
+P = 128
+TOK_TILES = 8
+KDIM = 2048
+ODIM = 2048
+RANK = 128
+PASSES = 4
+CHUNK = 512
+N_CHUNKS = 4
+N_OT = 16
+STEPS = 32
+PE_BIAS_BELOW = 18
+FIRST_ROUND = -8
+LEAD_H = 5
+LEAD_U = 3
+HP_FIRST = True
+LOAD_W = 2
+LOAD_H = 2
+LOAD_U = 2
+TR_BUFS = 4
+ACC_BUFS = 2
+TILE_ORDER = (0, 4, 1, 5, 2, 6, 3, 7)
+
+FLOPS = 2 * 1024 * ODIM * KDIM + 2 * 1024 * ODIM * RANK
+
+
+def tile_loratacmlp4_pb_kernel(tc, h, z, u, b, W_out_bytes, W_out_scale, b_out, out):
+    nc = tc.nc
+    with ExitStack() as ctx:
+        sb = ctx.enter_context(tc.tile_pool(name="sb", bufs=1))
+        ps = ctx.enter_context(tc.psum_pool(name="ps", bufs=2))
+        ctx.enter_context(tc.manual_schedule())
+
+        h_v = h.rearrange("b k f c -> (b k) f c")
+        out_v = out.rearrange("b k f n -> (b k) f n")
+        w_v = W_out_bytes.rearrange("(c a p) k -> c p a k", a=4, p=P)
+        u_v = u.rearrange("b k (c a p) r -> (b k) c p a r", c=N_CHUNKS, a=4, p=P)
+
+        wbytes = {}
+        wprod = {}
+        wgrp = {}
+        wcodes = {}
+        wscales = {}
+        hraw = {}
+        hgrp = {}
+        hcodes = {}
+        hscales = {}
+        uraw = {}
+        uT = {}
+        lora_ps = {}
+        acc_ps = {}
+        lsum = {}
+
+        def load_w(ot):
+            j, a = divmod(ot, 4)
+            if j not in wbytes:
+                wbytes[j] = sb.tile([P, 4, KDIM], U8, name="wbytes%d" % j, tag="wbytes", bufs=3)
+            nc.sync.dma_start(out=wbytes[j][:, a, :], in_=w_v[j][:, a, :])
+
+        def load_h(i):
+            hraw[i] = sb.tile([P, KDIM], BF16, name="hraw%d" % i, tag="hraw", bufs=4)
+            nc.sync.dma_start(out=hraw[i][:], in_=h_v[i])
+
+        def load_u(s):
+            j, m = s // TOK_TILES, TILE_ORDER[s % TOK_TILES]
+            uraw[s] = sb.tile([P, 4, RANK], BF16, name="uraw%d" % s, tag="uraw", bufs=8)
+            nc.sync.dma_start(out=uraw[s][:], in_=u_v[m][j])
+
+        sc_b = sb.tile([P, KDIM], F32, name="sc_b", tag="sc_b")
+        zraw = sb.tile([P, TOK_TILES, RANK], BF16, name="zraw", tag="zraw")
+        sc_col = sb.tile([P, KDIM // P], F32, name="sc_col", tag="sc_col")
+        nc.scalar.dma_start(out=sc_col[:], in_=W_out_scale.rearrange("o (p c) -> p (o c)", p=P))
+
+
+        warm = sb.tile([P, 2], F32, name="warm", tag="warm")
+        nc.vector.memset(warm[:], 0.0)
+        nc.scalar.activation(out=warm[:, 1:2], in_=warm[:, 0:1], func=ACT.Gelu)
+
+        ident_f = sb.tile([P, P], F32, name="ident_f", tag="ident_f")
+        make_identity(nc, ident_f[:])
+        ident_b = sb.tile([P, P], BF16, name="ident_b", tag="ident_b")
+        make_identity(nc, ident_b[:])
+        brow = sb.tile([P, 2, ODIM], BF16, name="brow", tag="brow")
+        nc.vector.memset(brow[:].rearrange("p b n -> p (b n)").bitcast(F32), 0.0)
+        ones = sb.tile([P, P], BF16, name="ones", tag="ones")
+        nc.vector.memset(ones[:], float(RANK))
+
+        bias = sb.tile([P, 2, ODIM], F32, name="bias", tag="bias")
+        zT = sb.tile([P, TOK_TILES, P], BF16, name="zT", tag="zT")
+
+        def spread_scales():
+            for g in range(4):
+                bank = ps.tile([P, 4, P], F32, name="sctr%d" % g, tag="tr", bufs=TR_BUFS)
+                for c in range(4):
+                    nc.tensor.transpose(bank[:, c, :], sc_col[:, 4 * g + c : 4 * g + c + 1].to_broadcast([P, P]), ident_f[:])
+                dst = sc_b[:].rearrange("p (n c) -> p n c", c=KDIM // P)[:, :, 4 * g : 4 * g + 4]
+                if g % 2 == 0:
+                    nc.scalar.copy(out=dst, in_=bank[:].rearrange("p c n -> p n c"))
+                else:
+                    nc.vector.tensor_copy(out=dst, in_=bank[:].rearrange("p c n -> p n c"))
+
+        def pe_bias(s):
+            return s < PE_BIAS_BELOW
+
+        def w_product(ot):
+            j, a = divmod(ot, 4)
+            wprod[ot] = sb.tile([P, KDIM], BF16, name="wprod%d" % ot, tag="wprod", bufs=4)
+            pieces = 1
+            width = KDIM // pieces
+            for c in range(pieces):
+                cols = slice(width * c, width * (c + 1))
+                nc.vector.tensor_tensor(
+                    out=wprod[ot][:, cols], in0=wbytes[j][:, a, cols].bitcast(FP8), in1=sc_b[:, cols], op=ALU.mult
+                )
+
+        def w_transpose(ot, gp):
+            pair, half = divmod(ot, 2)
+            if pair not in wgrp:
+                wgrp[pair] = sb.tile(
+                    [P, PASSES, 256, 4], BF16, name="wgrp%d" % pair, tag="wgrp", bufs=3, align_bytes=64
+                )
+            words = wprod[ot][:].bitcast(F32)
+            bank = ps.tile([P, 2, 2, P], F32, name="wtr%d_%d" % (ot, gp), tag="tr", bufs=TR_BUFS)
+            for gg in range(2):
+                g = 2 * gp + gg
+                for w in range(2):
+                    nc.tensor.transpose(bank[:, gg, w, :], words[:, 256 * g + w : 256 * (g + 1) : 2], ident_f[:])
+            nc.scalar.copy(
+                out=wgrp[pair][:].bitcast(F32)[:, 2 * gp : 2 * gp + 2, P * half : P * half + P, :],
+                in_=bank[:].rearrange("p g w o -> p g o w"),
+            )
+
+        def w_quantize(pair, g):
+            j, half = divmod(pair, 2)
+            if j not in wcodes:
+                wcodes[j] = sb.tile([P, PASSES, CHUNK], U32, name="wcodes%d" % j, tag="wcodes", bufs=2, align_bytes=64)
+                wscales[j] = sb.tile([P, PASSES, CHUNK], U8, name="wscales%d" % j, tag="wscales", bufs=2, align_bytes=64)
+            cols = slice(256 * half, 256 * half + 256)
+            nc.vector.quantize_mx(
+                out=wcodes[j][:, g, cols].bitcast(FP8X4),
+                scales=wscales[j][:, g, cols],
+                in_=wgrp[pair][:, g, :, :].rearrange("p o t -> p (o t)"),
+            )
+
+        def h_transpose(i):
+            hgrp[i] = sb.tile([P, PASSES, P, 4], BF16, name="hgrp%d" % i, tag="hgrp", bufs=4, align_bytes=64)
+            words = hraw[i][:].bitcast(F32)
+            for gp in range(2):
+                bank = ps.tile([P, 2, 2, P], F32, name="htr%d_%d" % (i, gp), tag="tr", bufs=TR_BUFS)
+                for gg in range(2):
+                    g = 2 * gp + gg
+                    for w in range(2):
+                        nc.tensor.transpose(bank[:, gg, w, :], words[:, 256 * g + w : 256 * (g + 1) : 2], ident_f[:])
+                nc.scalar.copy(
+                    out=hgrp[i][:].bitcast(F32)[:, 2 * gp : 2 * gp + 2, :, :],
+                    in_=bank[:].rearrange("p g w r -> p g r w"),
+                )
+
+        def h_quantize(i):
+            hcodes[i] = sb.tile([P, PASSES, P], U32, name="hcodes%d" % i, tag="hcodes%d" % i, align_bytes=64)
+            hscales[i] = sb.tile([P, PASSES, P], U8, name="hscales%d" % i, tag="hscales%d" % i, align_bytes=64)
+            nc.vector.quantize_mx(
+                out=hcodes[i][:].rearrange("p g r -> p (g r)").bitcast(FP8X4),
+                scales=hscales[i][:].rearrange("p g r -> p (g r)"),
+                in_=hgrp[i][:].rearrange("p g r t -> p (g r t)"),
+            )
+
+        def z_prep():
+            for half in range(2):
+                bank = ps.tile([P, 4, P], BF16, name="ztr%d" % half, tag="tr", bufs=TR_BUFS)
+                for m in range(4):
+                    nc.tensor.transpose(bank[:, m, :], zraw[:, 4 * half + m, :], ident_b[:])
+                nc.scalar.copy(out=zT[:, 4 * half : 4 * half + 4, :], in_=bank[:])
+
+        def bias_slice(bb, j):
+            cols = slice(CHUNK * j, CHUNK * (j + 1))
+            bank = ps.tile([P, CHUNK], F32, name="bps%d_%d" % (bb, j), tag="lp", bufs=2)
+            nc.tensor.matmul(bank[:], lhsT=ones[:], rhs=brow[:, bb, cols], start=True, stop=True)
+            nc.scalar.activation(out=bias[:, bb, cols], in_=bank[:], func=ACT.Copy, scale=1.0 / RANK)
+
+        def u_transpose(s):
+            j, n = divmod(s, TOK_TILES)
+            if j not in uT:
+                uT[j] = sb.tile([P, TOK_TILES, CHUNK], BF16, name="uT%d" % j, tag="uT", bufs=2)
+            bank = ps.tile([P, 2, 4, P], BF16, name="utr%d" % s, tag="tr", bufs=TR_BUFS)
+            for e in range(2):
+                for a in range(4):
+                    nc.tensor.transpose(bank[:, e, a, :], uraw[s + e][:, a, :], ident_b[:])
+            nc.scalar.copy(out=uT[j][:, n : n + 2, :], in_=bank[:].rearrange("p e a q -> p e (a q)"))
+
+        def lora_matmul(s):
+            j, i = s // TOK_TILES, TILE_ORDER[s % TOK_TILES]
+            lora_ps[s] = ps.tile([P, CHUNK], F32, name="lp%d" % s, tag="lp", bufs=2)
+            nc.tensor.matmul(lora_ps[s][:], lhsT=zT[:, i, :], rhs=uT[j][:, s % TOK_TILES, :], start=True, stop=not pe_bias(s))
+            if pe_bias(s):
+                nc.tensor.matmul(
+                    lora_ps[s][:], lhsT=ones[:], rhs=brow[:, i // 4, CHUNK * j : CHUNK * (j + 1)], start=False, stop=True
+                )
+
+        def lora_out(s):
+            j, i = s // TOK_TILES, TILE_ORDER[s % TOK_TILES]
+            lsum[s] = sb.tile([P, CHUNK], F32, name="lsum%d" % s, tag="lsum", bufs=4)
+            if pe_bias(s):
+                nc.scalar.activation(out=lsum[s][:], in_=lora_ps[s][:], func=ACT.Copy, scale=1.0 / RANK)
+                return
+            nc.vector.scalar_tensor_tensor(
+                out=lsum[s][:],
+                in0=lora_ps[s][:],
+                scalar=1.0 / RANK,
+                in1=bias[:, i // 4, CHUNK * j : CHUNK * (j + 1)],
+                op0=ALU.mult,
+                op1=ALU.add,
+            )
+
+        def main_matmul(s):
+            j, i = s // TOK_TILES, TILE_ORDER[s % TOK_TILES]
+            acc_ps[s] = ps.tile([P, CHUNK], F32, name="acc%d" % s, tag="acc", bufs=ACC_BUFS)
+            for g in range(PASSES):
+                nc.tensor.matmul_mx(
+                    out=acc_ps[s][:],
+                    lhsT=hcodes[i][:, g, :].bitcast(FP8X4),
+                    lhsT_scale=hscales[i][:, g, :],
+                    rhs=wcodes[j][:, g, :].bitcast(FP8X4),
+                    rhs_scale=wscales[j][:, g, :],
+                    start=(g == 0),
+                    stop=(g == PASSES - 1),
+                )
+
+        def finish(s):
+            j, i = s // TOK_TILES, TILE_ORDER[s % TOK_TILES]
+            total = sb.tile([P, CHUNK], F32, name="total%d" % s, tag="total", bufs=3)
+            nc.vector.tensor_tensor(out=total[:], in0=acc_ps[s][:], in1=lsum[s][:], op=ALU.add)
+            res = sb.tile([P, CHUNK], F32, name="res%d" % s, tag="res", bufs=4)
+            nc.scalar.activation(out=res[:], in_=total[:], func=ACT.Gelu)
+            nc.sync.dma_start(out=out_v[i][:, CHUNK * j : CHUNK * (j + 1)], in_=res[:])
+
+        def in_steps(s):
+            return 0 <= s < STEPS
+
+        def wt(ot):
+            w_transpose(ot, 0)
+            w_transpose(ot, 1)
+
+        made = set()
+        spread_scales()
+        for q in range(FIRST_ROUND, 16):
+            if 0 <= q + 5 < N_OT:
+                w_product(q + 5)
+            for s in (2 * q + 4, 2 * q + 5):
+                if in_steps(s) and not pe_bias(s):
+                    key = (TILE_ORDER[s % TOK_TILES] // 4, s // TOK_TILES)
+                    if key not in made:
+                        made.add(key)
+                        bias_slice(key[0], key[1])
+            if q >= 0:
+                main_matmul(2 * q)
+                main_matmul(2 * q + 1)
+            nxt = [s for s in (2 * q + 2, 2 * q + 3) if in_steps(s)]
+            for s in nxt:
+                lora_matmul(s)
+            if q >= 0:
+                finish(2 * q)
+                finish(2 * q + 1)
+            if (q + 3) % 2 == 0 and 0 <= (q + 3) // 2 < 8:
+                for g in range(PASSES):
+                    w_quantize((q + 3) // 2, g)
+            for s in nxt:
+                lora_out(s)
+            for n in (2 * (q + LEAD_H - 1), 2 * (q + LEAD_H - 1) + 1):
+                if 0 <= n < TOK_TILES:
+                    h_quantize(TILE_ORDER[n])
+            for n in (2 * (q + LEAD_H), 2 * (q + LEAD_H) + 1):
+                if 0 <= n < TOK_TILES and HP_FIRST:
+                    h_transpose(TILE_ORDER[n])
+            if 0 <= q + 5 < N_OT:
+                wt(q + 5)
+            if q == -1 - LEAD_U:
+                z_prep()
+            if in_steps(2 * (q + LEAD_U)):
+                u_transpose(2 * (q + LEAD_U))
+            for n in (2 * (q + LEAD_H), 2 * (q + LEAD_H) + 1):
+                if 0 <= n < TOK_TILES and not HP_FIRST:
+                    h_transpose(TILE_ORDER[n])
+            if 0 <= q + 5 + LOAD_W < N_OT:
+                load_w(q + 5 + LOAD_W)
+            for n in (2 * (q + LEAD_H + LOAD_H), 2 * (q + LEAD_H + LOAD_H) + 1):
+                if 0 <= n < TOK_TILES:
+                    load_h(TILE_ORDER[n])
+            if q == FIRST_ROUND + 2:
+                nc.sync.dma_start(out=zraw[:], in_=z.rearrange("b k f r -> f (b k) r"))
+                for bb in range(2):
+                    nc.sync.dma_start(out=brow[0:1, bb, :], in_=b_out.rearrange("(o n) -> o n", o=1))
+                nc.sync.dma_start(out=brow[1:2, :, :], in_=b.rearrange("b x y n -> (x y) b n"))
+            for s in (2 * (q + LEAD_U + LOAD_U), 2 * (q + LEAD_U + LOAD_U) + 1):
+                if in_steps(s):
+                    load_u(s)

@@ -82,7 +82,10 @@ def tile_loratacmlp4_pb_kernel(tc, h, z, u, b, W_out_bytes, W_out_scale, b_out, 
         sc_b = sb.tile([P, KDIM], F32, name="sc_b", tag="sc_b")
         zraw = sb.tile([P, TOK_TILES, RANK], BF16, name="zraw", tag="zraw")
         sc_col = sb.tile([P, KDIM // P], F32, name="sc_col", tag="sc_col")
-        nc.scalar.dma_start(out=sc_col[:], in_=W_out_scale.rearrange("o (p c) -> p (o c)", p=P))
+        nc.scalar.dma_start(
+            out=sc_col[:].rearrange("p (g c) -> p g c", c=4),
+            in_=W_out_scale.rearrange("o (g p c) -> p (o g) c", g=PASSES, p=P, c=4),
+        )
 
 
         warm = sb.tile([P, 2], F32, name="warm", tag="warm")
@@ -106,11 +109,8 @@ def tile_loratacmlp4_pb_kernel(tc, h, z, u, b, W_out_bytes, W_out_scale, b_out, 
                 bank = ps.tile([P, 4, P], F32, name="sctr%d" % g, tag="tr", bufs=TR_BUFS)
                 for c in range(4):
                     nc.tensor.transpose(bank[:, c, :], sc_col[:, 4 * g + c : 4 * g + c + 1].to_broadcast([P, P]), ident_f[:])
-                dst = sc_b[:].rearrange("p (n c) -> p n c", c=KDIM // P)[:, :, 4 * g : 4 * g + 4]
-                if g % 2 == 0:
-                    nc.scalar.copy(out=dst, in_=bank[:].rearrange("p c n -> p n c"))
-                else:
-                    nc.vector.tensor_copy(out=dst, in_=bank[:].rearrange("p c n -> p n c"))
+                dst = sc_b[:, 512 * g : 512 * (g + 1)].rearrange("p (n c) -> p n c", c=4)
+                nc.scalar.copy(out=dst, in_=bank[:].rearrange("p c n -> p n c"))
 
         def pe_bias(s):
             return s < PE_BIAS_BELOW
@@ -118,7 +118,7 @@ def tile_loratacmlp4_pb_kernel(tc, h, z, u, b, W_out_bytes, W_out_scale, b_out, 
         def w_product(ot):
             j, a = divmod(ot, 4)
             wprod[ot] = sb.tile([P, KDIM], BF16, name="wprod%d" % ot, tag="wprod", bufs=4)
-            pieces = 1
+            pieces = PASSES if ot == 0 else 1
             width = KDIM // pieces
             for c in range(pieces):
                 cols = slice(width * c, width * (c + 1))
@@ -183,7 +183,10 @@ def tile_loratacmlp4_pb_kernel(tc, h, z, u, b, W_out_bytes, W_out_scale, b_out, 
                 bank = ps.tile([P, 4, P], BF16, name="ztr%d" % half, tag="tr", bufs=TR_BUFS)
                 for m in range(4):
                     nc.tensor.transpose(bank[:, m, :], zraw[:, 4 * half + m, :], ident_b[:])
-                nc.scalar.copy(out=zT[:, 4 * half : 4 * half + 4, :], in_=bank[:])
+                nc.scalar.copy(
+                    out=zT[:, 4 * half : 4 * half + 4, :].rearrange("p m q -> p (m q)").bitcast(F32),
+                    in_=bank[:].rearrange("p m q -> p (m q)").bitcast(F32),
+                )
 
         def bias_slice(bb, j):
             cols = slice(CHUNK * j, CHUNK * (j + 1))
@@ -199,7 +202,10 @@ def tile_loratacmlp4_pb_kernel(tc, h, z, u, b, W_out_bytes, W_out_scale, b_out, 
             for e in range(2):
                 for a in range(4):
                     nc.tensor.transpose(bank[:, e, a, :], uraw[s + e][:, a, :], ident_b[:])
-            nc.scalar.copy(out=uT[j][:, n : n + 2, :], in_=bank[:].rearrange("p e a q -> p e (a q)"))
+            nc.scalar.copy(
+                out=uT[j][:, n : n + 2, :].rearrange("p e c -> p (e c)").bitcast(F32),
+                in_=bank[:].rearrange("p e a q -> p (e a q)").bitcast(F32),
+            )
 
         def lora_matmul(s):
             j, i = s // TOK_TILES, TILE_ORDER[s % TOK_TILES]
@@ -269,7 +275,7 @@ def tile_loratacmlp4_pb_kernel(tc, h, z, u, b, W_out_bytes, W_out_scale, b_out, 
                 main_matmul(2 * q)
                 main_matmul(2 * q + 1)
             nxt = [s for s in (2 * q + 2, 2 * q + 3) if in_steps(s)]
-            for s in nxt:
+            for s in nxt[:1]:
                 lora_matmul(s)
             if q >= 0:
                 finish(2 * q)
@@ -277,7 +283,7 @@ def tile_loratacmlp4_pb_kernel(tc, h, z, u, b, W_out_bytes, W_out_scale, b_out, 
             if (q + 3) % 2 == 0 and 0 <= (q + 3) // 2 < 8:
                 for g in range(PASSES):
                     w_quantize((q + 3) // 2, g)
-            for s in nxt:
+            for s in nxt[:1]:
                 lora_out(s)
             for n in (2 * (q + LEAD_H - 1), 2 * (q + LEAD_H - 1) + 1):
                 if 0 <= n < TOK_TILES:
@@ -294,6 +300,9 @@ def tile_loratacmlp4_pb_kernel(tc, h, z, u, b, W_out_bytes, W_out_scale, b_out, 
             for n in (2 * (q + LEAD_H), 2 * (q + LEAD_H) + 1):
                 if 0 <= n < TOK_TILES and not HP_FIRST:
                     h_transpose(TILE_ORDER[n])
+            for s in nxt[1:]:
+                lora_matmul(s)
+                lora_out(s)
             if 0 <= q + 5 + LOAD_W < N_OT:
                 load_w(q + 5 + LOAD_W)
             for n in (2 * (q + LEAD_H + LOAD_H), 2 * (q + LEAD_H + LOAD_H) + 1):

@@ -19,6 +19,7 @@ ODIM = 2048
 RANK = 128
 PASSES = 4
 CHUNK = 512
+HALF = 256
 N_CHUNKS = 4
 N_OT = 16
 STEPS = 32
@@ -63,6 +64,7 @@ def tile_loratacmlp4_pb_kernel(tc, h, z, u, b, W_out_bytes, W_out_scale, b_out, 
         lora_ps = {}
         acc_ps = {}
         lsum = {}
+        acc_half = {}
 
         def load_w(ot):
             j, a = divmod(ot, 4)
@@ -253,6 +255,30 @@ def tile_loratacmlp4_pb_kernel(tc, h, z, u, b, W_out_bytes, W_out_scale, b_out, 
             nc.scalar.activation(out=res[:], in_=total[:], func=ACT.Gelu)
             nc.sync.dma_start(out=out_v[i][:, CHUNK * j : CHUNK * (j + 1)], in_=res[:])
 
+        def main_half(s, part):
+            j, i = s // TOK_TILES, TILE_ORDER[s % TOK_TILES]
+            cols = slice(HALF * part, HALF * (part + 1))
+            acc_half[part] = ps.tile([P, HALF], F32, name="acch%d" % part, tag="acc" if part == 0 else "lp", bufs=2)
+            for g in range(PASSES):
+                nc.tensor.matmul_mx(
+                    out=acc_half[part][:],
+                    lhsT=hcodes[i][:, g, :].bitcast(FP8X4),
+                    lhsT_scale=hscales[i][:, g, :],
+                    rhs=wcodes[j][:, g, cols].bitcast(FP8X4),
+                    rhs_scale=wscales[j][:, g, cols],
+                    start=(g == 0),
+                    stop=(g == PASSES - 1),
+                )
+
+        def finish_half(s, part):
+            j, i = s // TOK_TILES, TILE_ORDER[s % TOK_TILES]
+            cols = slice(HALF * part, HALF * (part + 1))
+            total = sb.tile([P, HALF], F32, name="totalh%d" % part, tag="total", bufs=3)
+            nc.vector.tensor_tensor(out=total[:], in0=acc_half[part][:], in1=lsum[s][:, cols], op=ALU.add)
+            res = sb.tile([P, HALF], F32, name="resh%d" % part, tag="res", bufs=4)
+            nc.scalar.activation(out=res[:], in_=total[:], func=ACT.Gelu)
+            nc.sync.dma_start(out=out_v[i][:, CHUNK * j + HALF * part : CHUNK * j + HALF * (part + 1)], in_=res[:])
+
         def in_steps(s):
             return 0 <= s < STEPS
 
@@ -273,13 +299,21 @@ def tile_loratacmlp4_pb_kernel(tc, h, z, u, b, W_out_bytes, W_out_scale, b_out, 
                         bias_slice(key[0], key[1])
             if q >= 0:
                 main_matmul(2 * q)
-                main_matmul(2 * q + 1)
+                if 2 * q + 1 < STEPS - 1:
+                    main_matmul(2 * q + 1)
+                else:
+                    main_half(2 * q + 1, 0)
+                    main_half(2 * q + 1, 1)
             nxt = [s for s in (2 * q + 2, 2 * q + 3) if in_steps(s)]
             for s in nxt[:1]:
                 lora_matmul(s)
             if q >= 0:
                 finish(2 * q)
-                finish(2 * q + 1)
+                if 2 * q + 1 < STEPS - 1:
+                    finish(2 * q + 1)
+                else:
+                    finish_half(2 * q + 1, 0)
+                    finish_half(2 * q + 1, 1)
             if (q + 3) % 2 == 0 and 0 <= (q + 3) // 2 < 8:
                 for g in range(PASSES):
                     w_quantize((q + 3) // 2, g)
@@ -291,12 +325,12 @@ def tile_loratacmlp4_pb_kernel(tc, h, z, u, b, W_out_bytes, W_out_scale, b_out, 
             for n in (2 * (q + LEAD_H), 2 * (q + LEAD_H) + 1):
                 if 0 <= n < TOK_TILES and HP_FIRST:
                     h_transpose(TILE_ORDER[n])
-            if 0 <= q + 5 < N_OT:
-                wt(q + 5)
             if q == -1 - LEAD_U:
                 z_prep()
             if in_steps(2 * (q + LEAD_U)):
                 u_transpose(2 * (q + LEAD_U))
+            if 0 <= q + 5 < N_OT:
+                wt(q + 5)
             for n in (2 * (q + LEAD_H), 2 * (q + LEAD_H) + 1):
                 if 0 <= n < TOK_TILES and not HP_FIRST:
                     h_transpose(TILE_ORDER[n])

@@ -325,12 +325,12 @@ def tile_loratacmlp4_pb_kernel(tc, h, z, u, b, W_out_bytes, W_out_scale, b_out, 
             for n in (2 * (q + LEAD_H), 2 * (q + LEAD_H) + 1):
                 if 0 <= n < TOK_TILES and HP_FIRST:
                     h_transpose(TILE_ORDER[n])
+            if 0 <= q + 5 < N_OT:
+                wt(q + 5)
             if q == -1 - LEAD_U:
                 z_prep()
             if in_steps(2 * (q + LEAD_U)):
                 u_transpose(2 * (q + LEAD_U))
-            if 0 <= q + 5 < N_OT:
-                wt(q + 5)
             for n in (2 * (q + LEAD_H), 2 * (q + LEAD_H) + 1):
                 if 0 <= n < TOK_TILES and not HP_FIRST:
                     h_transpose(TILE_ORDER[n])

@@ -28,7 +28,7 @@ FIRST_ROUND = -8
 LEAD_H = 5
 LEAD_U = 3
 HP_FIRST = True
-LOAD_W = 2
+LOAD_W = 3
 LOAD_H = 2
 LOAD_U = 2
 TR_BUFS = 4

@@ -27,6 +27,7 @@ PE_BIAS_BELOW = 18
 FIRST_ROUND = -8
 LEAD_H = 5
 LEAD_U = 3
+BF16_FROM = -2
 HP_FIRST = True
 LOAD_W = 3
 LOAD_H = 2
@@ -327,10 +328,11 @@ def tile_loratacmlp4_pb_kernel(tc, h, z, u, b, W_out_bytes, W_out_scale, b_out, 
                     h_transpose(TILE_ORDER[n])
             if 0 <= q + 5 < N_OT:
                 wt(q + 5)
-            if q == -1 - LEAD_U:
+            if q == BF16_FROM:
                 z_prep()
-            if in_steps(2 * (q + LEAD_U)):
-                u_transpose(2 * (q + LEAD_U))
+            for s in range(0, STEPS, 2):
+                if max(s // 2 - LEAD_U, BF16_FROM) == q:
+                    u_transpose(s)
             for n in (2 * (q + LEAD_H), 2 * (q + LEAD_H) + 1):
                 if 0 <= n < TOK_TILES and not HP_FIRST:
                     h_transpose(TILE_ORDER[n])
@@ -342,11 +344,11 @@ def tile_loratacmlp4_pb_kernel(tc, h, z, u, b, W_out_bytes, W_out_scale, b_out, 
             for n in (2 * (q + LEAD_H + LOAD_H), 2 * (q + LEAD_H + LOAD_H) + 1):
                 if 0 <= n < TOK_TILES:
                     load_h(TILE_ORDER[n])
-            if q == FIRST_ROUND + 2:
+            if q == BF16_FROM - LOAD_U:
                 nc.sync.dma_start(out=zraw[:], in_=z.rearrange("b k f r -> f (b k) r"))
                 for bb in range(2):
                     nc.sync.dma_start(out=brow[0:1, bb, :], in_=b_out.rearrange("(o n) -> o n", o=1))
                 nc.sync.dma_start(out=brow[1:2, :, :], in_=b.rearrange("b x y n -> (x y) b n"))
-            for s in (2 * (q + LEAD_U + LOAD_U), 2 * (q + LEAD_U + LOAD_U) + 1):
-                if in_steps(s):
+            for s in range(STEPS):
+                if max(s // 2 - LEAD_U, BF16_FROM) - LOAD_U == q:
                     load_u(s)

@@ -23,17 +23,25 @@ HALF = 256
 N_CHUNKS = 4
 N_OT = 16
 STEPS = 32
-PE_BIAS_BELOW = 18
-FIRST_ROUND = -8
+FIRST_ROUND = -9
+LEAD_W = 5
 LEAD_H = 5
-LEAD_U = 3
-BF16_FROM = -2
-HP_FIRST = True
-LOAD_W = 3
+LEAD_U = 4
+LEAD_C = 1
+LEAD_L = 2
+V_FROM = 22
+BF16_FROM = -3
+LOAD_W = 4
 LOAD_H = 2
 LOAD_U = 2
+LOAD_B = 6
+MAKE_B = 3
 TR_BUFS = 4
 ACC_BUFS = 2
+LP_BUFS = 2
+VC_FROM = 1
+LOADS_FIRST_FROM = 0
+VC_TO = 12
 TILE_ORDER = (0, 4, 1, 5, 2, 6, 3, 7)
 
 FLOPS = 2 * 1024 * ODIM * KDIM + 2 * 1024 * ODIM * RANK
@@ -50,9 +58,10 @@ def tile_loratacmlp4_pb_kernel(tc, h, z, u, b, W_out_bytes, W_out_scale, b_out, 
         out_v = out.rearrange("b k f n -> (b k) f n")
         w_v = W_out_bytes.rearrange("(c a p) k -> c p a k", a=4, p=P)
         u_v = u.rearrange("b k (c a p) r -> (b k) c p a r", c=N_CHUNKS, a=4, p=P)
+        b_v = b.rearrange("b x y n -> (b x y) n")
 
         wbytes = {}
-        wprod = {}
+        wcast = {}
         wgrp = {}
         wcodes = {}
         wscales = {}
@@ -66,11 +75,16 @@ def tile_loratacmlp4_pb_kernel(tc, h, z, u, b, W_out_bytes, W_out_scale, b_out, 
         acc_ps = {}
         lsum = {}
         acc_half = {}
+        banks = {}
 
         def load_w(ot):
             j, a = divmod(ot, 4)
             if j not in wbytes:
                 wbytes[j] = sb.tile([P, 4, KDIM], U8, name="wbytes%d" % j, tag="wbytes", bufs=3)
+            if ot < 2:
+                cols = slice(KDIM // 2 * ot, KDIM // 2 * (ot + 1))
+                nc.sync.dma_start(out=wbytes[0][:, 0:2, cols], in_=w_v[0][:, 0:2, cols])
+                return
             nc.sync.dma_start(out=wbytes[j][:, a, :], in_=w_v[j][:, a, :])
 
         def load_h(i):
@@ -82,14 +96,12 @@ def tile_loratacmlp4_pb_kernel(tc, h, z, u, b, W_out_bytes, W_out_scale, b_out, 
             uraw[s] = sb.tile([P, 4, RANK], BF16, name="uraw%d" % s, tag="uraw", bufs=8)
             nc.sync.dma_start(out=uraw[s][:], in_=u_v[m][j])
 
-        sc_b = sb.tile([P, KDIM], F32, name="sc_b", tag="sc_b")
         zraw = sb.tile([P, TOK_TILES, RANK], BF16, name="zraw", tag="zraw")
         sc_col = sb.tile([P, KDIM // P], F32, name="sc_col", tag="sc_col")
         nc.scalar.dma_start(
             out=sc_col[:].rearrange("p (g c) -> p g c", c=4),
             in_=W_out_scale.rearrange("o (g p c) -> p (o g) c", g=PASSES, p=P, c=4),
         )
-
 
         warm = sb.tile([P, 2], F32, name="warm", tag="warm")
         nc.vector.memset(warm[:], 0.0)
@@ -99,51 +111,64 @@ def tile_loratacmlp4_pb_kernel(tc, h, z, u, b, W_out_bytes, W_out_scale, b_out, 
         make_identity(nc, ident_f[:])
         ident_b = sb.tile([P, P], BF16, name="ident_b", tag="ident_b")
         make_identity(nc, ident_b[:])
-        brow = sb.tile([P, 2, ODIM], BF16, name="brow", tag="brow")
-        nc.vector.memset(brow[:].rearrange("p b n -> p (b n)").bitcast(F32), 0.0)
-        ones = sb.tile([P, P], BF16, name="ones", tag="ones")
-        nc.vector.memset(ones[:], float(RANK))
 
-        bias = sb.tile([P, 2, ODIM], F32, name="bias", tag="bias")
+        bias = sb.tile([P, N_CHUNKS, 2, CHUNK], F32, name="bias", tag="bias")
         zT = sb.tile([P, TOK_TILES, P], BF16, name="zT", tag="zT")
+        brow = {}
 
-        def spread_scales():
-            for g in range(4):
-                bank = ps.tile([P, 4, P], F32, name="sctr%d" % g, tag="tr", bufs=TR_BUFS)
-                for c in range(4):
-                    nc.tensor.transpose(bank[:, c, :], sc_col[:, 4 * g + c : 4 * g + c + 1].to_broadcast([P, P]), ident_f[:])
-                dst = sc_b[:, 512 * g : 512 * (g + 1)].rearrange("p (n c) -> p n c", c=4)
-                nc.scalar.copy(out=dst, in_=bank[:].rearrange("p c n -> p n c"))
+        def load_bias(j):
+            cols = slice(CHUNK * j, CHUNK * (j + 1))
+            brow[j] = sb.tile([P, 3, CHUNK], BF16, name="brow%d" % j, tag="brow", bufs=2)
+            nc.sync.dma_start(out=brow[j][:, 0, :], in_=b_out[cols].partition_broadcast(P))
+            for bb in range(2):
+                nc.sync.dma_start(out=brow[j][:, 1 + bb, :], in_=b_v[bb, cols].partition_broadcast(P))
 
-        def pe_bias(s):
-            return s < PE_BIAS_BELOW
+        def make_bias(j):
+            for bb in range(2):
+                nc.gpsimd.tensor_tensor(out=bias[:, j, bb, :], in0=brow[j][:, 1 + bb, :], in1=brow[j][:, 0, :], op=ALU.add)
 
-        def w_product(ot):
-            j, a = divmod(ot, 4)
-            wprod[ot] = sb.tile([P, KDIM], BF16, name="wprod%d" % ot, tag="wprod", bufs=4)
-            pieces = PASSES if ot == 0 else 1
-            width = KDIM // pieces
+        def v_cast(ot, part):
+            return ot == 0 or VC_FROM <= ot < VC_TO and part == 1
+
+        def v_lora(s):
+            return s >= V_FROM
+
+        def w_cast(t, a):
+            pair, gp = divmod(t, 2)
+            j, lo = divmod(2 * pair + a, 4)
+            if a == 0:
+                wcast[t] = sb.tile([P, 2, KDIM // 2], BF16, name="wcast%d" % t, tag="wcast", bufs=3)
+            pieces = 2 if t == 0 else 1
+            width = KDIM // 2 // pieces
             for c in range(pieces):
-                cols = slice(width * c, width * (c + 1))
-                nc.vector.tensor_tensor(
-                    out=wprod[ot][:, cols], in0=wbytes[j][:, a, cols].bitcast(FP8), in1=sc_b[:, cols], op=ALU.mult
-                )
+                dst = wcast[t][:, a, width * c : width * (c + 1)]
+                src = wbytes[j][:, lo, KDIM // 2 * gp + width * c : KDIM // 2 * gp + width * (c + 1)].bitcast(FP8)
+                if v_cast(t, a):
+                    nc.vector.tensor_copy(out=dst, in_=src)
+                else:
+                    nc.scalar.copy(out=dst, in_=src)
 
-        def w_transpose(ot, gp):
-            pair, half = divmod(ot, 2)
+        def w_transpose(t, gg):
+            words = wcast[t][:].rearrange("p a k -> p (a k)").bitcast(F32)
+            bank = ps.tile([P, 2, 256], F32, name="wtr%d_%d" % (t, gg), tag="tr", bufs=TR_BUFS)
+            for a in range(2):
+                for w in range(2):
+                    first = 512 * a + 256 * gg + w
+                    nc.tensor.transpose(bank[:, w, P * a : P * (a + 1)], words[:, first : first - w + 256 : 2], ident_f[:])
+            banks[t, gg] = bank
+
+        def w_scale(t, gg):
+            pair, gp = divmod(t, 2)
+            g = 2 * gp + gg
             if pair not in wgrp:
                 wgrp[pair] = sb.tile(
                     [P, PASSES, 256, 4], BF16, name="wgrp%d" % pair, tag="wgrp", bufs=3, align_bytes=64
                 )
-            words = wprod[ot][:].bitcast(F32)
-            bank = ps.tile([P, 2, 2, P], F32, name="wtr%d_%d" % (ot, gp), tag="tr", bufs=TR_BUFS)
-            for gg in range(2):
-                g = 2 * gp + gg
-                for w in range(2):
-                    nc.tensor.transpose(bank[:, gg, w, :], words[:, 256 * g + w : 256 * (g + 1) : 2], ident_f[:])
-            nc.scalar.copy(
-                out=wgrp[pair][:].bitcast(F32)[:, 2 * gp : 2 * gp + 2, P * half : P * half + P, :],
-                in_=bank[:].rearrange("p g w o -> p g o w"),
+            nc.vector.tensor_tensor(
+                out=wgrp[pair][:, g, :, :].rearrange("p o (w e) -> p o w e", e=2),
+                in0=banks[t, gg][:].bitcast(BF16).rearrange("p w (o e) -> p o w e", e=2),
+                in1=sc_col[:, 4 * g : 4 * g + 4].rearrange("p (w e) -> p w e", e=2).unsqueeze(1).to_broadcast([P, 256, 2, 2]),
+                op=ALU.mult,
             )
 
         def w_quantize(pair, g):
@@ -162,7 +187,7 @@ def tile_loratacmlp4_pb_kernel(tc, h, z, u, b, W_out_bytes, W_out_scale, b_out, 
             hgrp[i] = sb.tile([P, PASSES, P, 4], BF16, name="hgrp%d" % i, tag="hgrp", bufs=4, align_bytes=64)
             words = hraw[i][:].bitcast(F32)
             for gp in range(2):
-                bank = ps.tile([P, 2, 2, P], F32, name="htr%d_%d" % (i, gp), tag="tr", bufs=TR_BUFS)
+                bank = ps.tile([P, 2, 2, P], F32, name="htr%d_%d" % (i, gp), tag=("acc", "lp")[gp], bufs=2)
                 for gg in range(2):
                     g = 2 * gp + gg
                     for w in range(2):
@@ -183,19 +208,13 @@ def tile_loratacmlp4_pb_kernel(tc, h, z, u, b, W_out_bytes, W_out_scale, b_out, 
 
         def z_prep():
             for half in range(2):
-                bank = ps.tile([P, 4, P], BF16, name="ztr%d" % half, tag="tr", bufs=TR_BUFS)
+                bank = ps.tile([P, 4, P], BF16, name="ztr%d" % half, tag="acc", bufs=2)
                 for m in range(4):
                     nc.tensor.transpose(bank[:, m, :], zraw[:, 4 * half + m, :], ident_b[:])
                 nc.scalar.copy(
                     out=zT[:, 4 * half : 4 * half + 4, :].rearrange("p m q -> p (m q)").bitcast(F32),
                     in_=bank[:].rearrange("p m q -> p (m q)").bitcast(F32),
                 )
-
-        def bias_slice(bb, j):
-            cols = slice(CHUNK * j, CHUNK * (j + 1))
-            bank = ps.tile([P, CHUNK], F32, name="bps%d_%d" % (bb, j), tag="lp", bufs=2)
-            nc.tensor.matmul(bank[:], lhsT=ones[:], rhs=brow[:, bb, cols], start=True, stop=True)
-            nc.scalar.activation(out=bias[:, bb, cols], in_=bank[:], func=ACT.Copy, scale=1.0 / RANK)
 
         def u_transpose(s):
             j, n = divmod(s, TOK_TILES)
@@ -205,34 +224,35 @@ def tile_loratacmlp4_pb_kernel(tc, h, z, u, b, W_out_bytes, W_out_scale, b_out, 
             for e in range(2):
                 for a in range(4):
                     nc.tensor.transpose(bank[:, e, a, :], uraw[s + e][:, a, :], ident_b[:])
+            banks["u", s] = bank
+
+        def u_copy(s):
+            j, n = divmod(s, TOK_TILES)
             nc.scalar.copy(
                 out=uT[j][:, n : n + 2, :].rearrange("p e c -> p (e c)").bitcast(F32),
-                in_=bank[:].rearrange("p e a q -> p (e a q)").bitcast(F32),
+                in_=banks["u", s][:].rearrange("p e a q -> p (e a q)").bitcast(F32),
             )
 
         def lora_matmul(s):
             j, i = s // TOK_TILES, TILE_ORDER[s % TOK_TILES]
-            lora_ps[s] = ps.tile([P, CHUNK], F32, name="lp%d" % s, tag="lp", bufs=2)
-            nc.tensor.matmul(lora_ps[s][:], lhsT=zT[:, i, :], rhs=uT[j][:, s % TOK_TILES, :], start=True, stop=not pe_bias(s))
-            if pe_bias(s):
-                nc.tensor.matmul(
-                    lora_ps[s][:], lhsT=ones[:], rhs=brow[:, i // 4, CHUNK * j : CHUNK * (j + 1)], start=False, stop=True
-                )
+            lora_ps[s] = ps.tile([P, CHUNK], F32, name="lp%d" % s, tag="lp", bufs=LP_BUFS)
+            nc.tensor.matmul(lora_ps[s][:], lhsT=zT[:, i, :], rhs=uT[j][:, s % TOK_TILES, :], start=True, stop=True)
 
         def lora_out(s):
             j, i = s // TOK_TILES, TILE_ORDER[s % TOK_TILES]
-            lsum[s] = sb.tile([P, CHUNK], F32, name="lsum%d" % s, tag="lsum", bufs=4)
-            if pe_bias(s):
-                nc.scalar.activation(out=lsum[s][:], in_=lora_ps[s][:], func=ACT.Copy, scale=1.0 / RANK)
+            lsum[s] = sb.tile([P, CHUNK], F32, name="lsum%d" % s, tag="lsum", bufs=6)
+            if v_lora(s):
+                nc.vector.scalar_tensor_tensor(
+                    out=lsum[s][:],
+                    in0=lora_ps[s][:],
+                    scalar=1.0 / RANK,
+                    in1=bias[:, j, i // 4, :],
+                    op0=ALU.mult,
+                    op1=ALU.add,
+                )
                 return
-            nc.vector.scalar_tensor_tensor(
-                out=lsum[s][:],
-                in0=lora_ps[s][:],
-                scalar=1.0 / RANK,
-                in1=bias[:, i // 4, CHUNK * j : CHUNK * (j + 1)],
-                op0=ALU.mult,
-                op1=ALU.add,
-            )
+            nc.scalar.activation(out=lsum[s][:], in_=lora_ps[s][:], func=ACT.Copy, scale=1.0 / RANK)
+            nc.gpsimd.tensor_tensor(out=lsum[s][:], in0=lsum[s][:], in1=bias[:, j, i // 4, :], op=ALU.add)
 
         def main_matmul(s):
             j, i = s // TOK_TILES, TILE_ORDER[s % TOK_TILES]
@@ -283,21 +303,37 @@ def tile_loratacmlp4_pb_kernel(tc, h, z, u, b, W_out_bytes, W_out_scale, b_out, 
         def in_steps(s):
             return 0 <= s < STEPS
 
-        def wt(ot):
-            w_transpose(ot, 0)
-            w_transpose(ot, 1)
+        def u_round(q):
+            return [s for s in range(0, STEPS, 2) if max(s // 2 - LEAD_U, BF16_FROM) == q]
 
-        made = set()
-        spread_scales()
+        def loads(q, ot):
+            if 0 <= ot + LOAD_W < N_OT:
+                load_w(ot + LOAD_W)
+            for n in (2 * (q + LEAD_H + LOAD_H), 2 * (q + LEAD_H + LOAD_H) + 1):
+                if 0 <= n < TOK_TILES:
+                    load_h(TILE_ORDER[n])
+            if q == BF16_FROM - LOAD_U:
+                nc.sync.dma_start(out=zraw[:], in_=z.rearrange("b k f r -> f (b k) r"))
+            for j in range(N_CHUNKS):
+                if q == 4 * j - LOAD_B:
+                    load_bias(j)
+                if q == 4 * j - MAKE_B:
+                    make_bias(j)
+            for s in range(STEPS):
+                if max(s // 2 - LEAD_U, BF16_FROM) - LOAD_U == q:
+                    load_u(s)
+
         for q in range(FIRST_ROUND, 16):
-            if 0 <= q + 5 < N_OT:
-                w_product(q + 5)
-            for s in (2 * q + 4, 2 * q + 5):
-                if in_steps(s) and not pe_bias(s):
-                    key = (TILE_ORDER[s % TOK_TILES] // 4, s // TOK_TILES)
-                    if key not in made:
-                        made.add(key)
-                        bias_slice(key[0], key[1])
+            ot = q + LEAD_W
+            if q >= LOADS_FIRST_FROM:
+                loads(q, ot)
+            for s in u_round(q - 1):
+                u_copy(s)
+            if 0 <= ot - 1 < N_OT:
+                w_scale(ot - 1, 0)
+                w_scale(ot - 1, 1)
+            if in_steps(2 * (q - 1 + LEAD_L) + 1):
+                lora_out(2 * (q - 1 + LEAD_L) + 1)
             if q >= 0:
                 main_matmul(2 * q)
                 if 2 * q + 1 < STEPS - 1:
@@ -305,9 +341,8 @@ def tile_loratacmlp4_pb_kernel(tc, h, z, u, b, W_out_bytes, W_out_scale, b_out, 
                 else:
                     main_half(2 * q + 1, 0)
                     main_half(2 * q + 1, 1)
-            nxt = [s for s in (2 * q + 2, 2 * q + 3) if in_steps(s)]
-            for s in nxt[:1]:
-                lora_matmul(s)
+            if 0 <= ot + LEAD_C < N_OT:
+                w_cast(ot + LEAD_C, 0)
             if q >= 0:
                 finish(2 * q)
                 if 2 * q + 1 < STEPS - 1:
@@ -315,40 +350,31 @@ def tile_loratacmlp4_pb_kernel(tc, h, z, u, b, W_out_bytes, W_out_scale, b_out, 
                 else:
                     finish_half(2 * q + 1, 0)
                     finish_half(2 * q + 1, 1)
-            if (q + 3) % 2 == 0 and 0 <= (q + 3) // 2 < 8:
-                for g in range(PASSES):
-                    w_quantize((q + 3) // 2, g)
-            for s in nxt[:1]:
-                lora_out(s)
+            if in_steps(2 * (q + LEAD_L)):
+                lora_matmul(2 * (q + LEAD_L))
+            if 1 <= ot < N_OT + 1:
+                for gg in range(2):
+                    w_quantize((ot - 1) // 2, 2 * ((ot - 1) % 2) + gg)
             for n in (2 * (q + LEAD_H - 1), 2 * (q + LEAD_H - 1) + 1):
                 if 0 <= n < TOK_TILES:
                     h_quantize(TILE_ORDER[n])
+            if in_steps(2 * (q + LEAD_L)):
+                lora_out(2 * (q + LEAD_L))
+            if 0 <= ot < N_OT:
+                w_transpose(ot, 0)
+                w_transpose(ot, 1)
             for n in (2 * (q + LEAD_H), 2 * (q + LEAD_H) + 1):
-                if 0 <= n < TOK_TILES and HP_FIRST:
+                if 0 <= n < TOK_TILES:
                     h_transpose(TILE_ORDER[n])
-            if 0 <= q + 5 < N_OT:
-                wt(q + 5)
             if q == BF16_FROM:
                 z_prep()
-            for s in range(0, STEPS, 2):
-                if max(s // 2 - LEAD_U, BF16_FROM) == q:
-                    u_transpose(s)
-            for n in (2 * (q + LEAD_H), 2 * (q + LEAD_H) + 1):
-                if 0 <= n < TOK_TILES and not HP_FIRST:
-                    h_transpose(TILE_ORDER[n])
-            for s in nxt[1:]:
-                lora_matmul(s)
-                lora_out(s)
-            if 0 <= q + 5 + LOAD_W < N_OT:
-                load_w(q + 5 + LOAD_W)
-            for n in (2 * (q + LEAD_H + LOAD_H), 2 * (q + LEAD_H + LOAD_H) + 1):
-                if 0 <= n < TOK_TILES:
-                    load_h(TILE_ORDER[n])
-            if q == BF16_FROM - LOAD_U:
-                nc.sync.dma_start(out=zraw[:], in_=z.rearrange("b k f r -> f (b k) r"))
-                for bb in range(2):
-                    nc.sync.dma_start(out=brow[0:1, bb, :], in_=b_out.rearrange("(o n) -> o n", o=1))
-                nc.sync.dma_start(out=brow[1:2, :, :], in_=b.rearrange("b x y n -> (x y) b n"))
-            for s in range(STEPS):
-                if max(s // 2 - LEAD_U, BF16_FROM) - LOAD_U == q:
-                    load_u(s)
+            for s in u_round(q):
+                u_transpose(s)
+            if in_steps(2 * (q + LEAD_L) + 1):
+                lora_matmul(2 * (q + LEAD_L) + 1)
+            if 0 <= ot + LEAD_C < N_OT:
+                w_cast(ot + LEAD_C, 1)
+            if q < LOADS_FIRST_FROM - 1:
+                loads(q, ot)
+            if q == LOADS_FIRST_FROM - 1:
+                loads(q, ot)

@@ -112,7 +112,12 @@ def tile_loratacmlp4_pb_kernel(tc, h, z, u, b, W_out_bytes, W_out_scale, b_out, 
         ident_b = sb.tile([P, P], BF16, name="ident_b", tag="ident_b")
         make_identity(nc, ident_b[:])
 
-        bias = sb.tile([P, N_CHUNKS, 2, CHUNK], F32, name="bias", tag="bias")
+        ones = sb.tile([P, P], BF16, name="ones", tag="ones")
+        nc.vector.memset(ones[:], float(RANK))
+        rows = sb.tile([P, 2, ODIM], BF16, name="rows", tag="rows")
+        nc.vector.memset(rows[:].rearrange("p b n -> p (b n)").bitcast(F32), 0.0)
+
+        bias = sb.tile([P, 2, 2, CHUNK], F32, name="bias", tag="bias")
         zT = sb.tile([P, TOK_TILES, P], BF16, name="zT", tag="zT")
         brow = {}
 
@@ -125,7 +130,7 @@ def tile_loratacmlp4_pb_kernel(tc, h, z, u, b, W_out_bytes, W_out_scale, b_out, 
 
         def make_bias(j):
             for bb in range(2):
-                nc.gpsimd.tensor_tensor(out=bias[:, j, bb, :], in0=brow[j][:, 1 + bb, :], in1=brow[j][:, 0, :], op=ALU.add)
+                nc.gpsimd.tensor_tensor(out=bias[:, j - 2, bb, :], in0=brow[j][:, 1 + bb, :], in1=brow[j][:, 0, :], op=ALU.add)
 
         def v_cast(ot, part):
             return ot == 0 or VC_FROM <= ot < VC_TO and part == 1
@@ -236,7 +241,11 @@ def tile_loratacmlp4_pb_kernel(tc, h, z, u, b, W_out_bytes, W_out_scale, b_out, 
         def lora_matmul(s):
             j, i = s // TOK_TILES, TILE_ORDER[s % TOK_TILES]
             lora_ps[s] = ps.tile([P, CHUNK], F32, name="lp%d" % s, tag="lp", bufs=LP_BUFS)
-            nc.tensor.matmul(lora_ps[s][:], lhsT=zT[:, i, :], rhs=uT[j][:, s % TOK_TILES, :], start=True, stop=True)
+            nc.tensor.matmul(lora_ps[s][:], lhsT=zT[:, i, :], rhs=uT[j][:, s % TOK_TILES, :], start=True, stop=v_lora(s))
+            if not v_lora(s):
+                nc.tensor.matmul(
+                    lora_ps[s][:], lhsT=ones[:], rhs=rows[:, i // 4, CHUNK * j : CHUNK * (j + 1)], start=False, stop=True
+                )
 
         def lora_out(s):
             j, i = s // TOK_TILES, TILE_ORDER[s % TOK_TILES]
@@ -246,13 +255,12 @@ def tile_loratacmlp4_pb_kernel(tc, h, z, u, b, W_out_bytes, W_out_scale, b_out, 
                     out=lsum[s][:],
                     in0=lora_ps[s][:],
                     scalar=1.0 / RANK,
-                    in1=bias[:, j, i // 4, :],
+                    in1=bias[:, j - 2, i // 4, :],
                     op0=ALU.mult,
                     op1=ALU.add,
                 )
                 return
             nc.scalar.activation(out=lsum[s][:], in_=lora_ps[s][:], func=ACT.Copy, scale=1.0 / RANK)
-            nc.gpsimd.tensor_tensor(out=lsum[s][:], in0=lsum[s][:], in1=bias[:, j, i // 4, :], op=ALU.add)
 
         def main_matmul(s):
             j, i = s // TOK_TILES, TILE_ORDER[s % TOK_TILES]
@@ -314,7 +322,10 @@ def tile_loratacmlp4_pb_kernel(tc, h, z, u, b, W_out_bytes, W_out_scale, b_out, 
                     load_h(TILE_ORDER[n])
             if q == BF16_FROM - LOAD_U:
                 nc.sync.dma_start(out=zraw[:], in_=z.rearrange("b k f r -> f (b k) r"))
-            for j in range(N_CHUNKS):
+                for bb in range(2):
+                    nc.sync.dma_start(out=rows[0:1, bb, :], in_=b_out.rearrange("(o n) -> o n", o=1))
+                nc.sync.dma_start(out=rows[1:2, :, :], in_=b.rearrange("b x y n -> (x y) b n"))
+            for j in (2, 3):
                 if q == 4 * j - LOAD_B:
                     load_bias(j)
                 if q == 4 * j - MAKE_B:

@@ -28,8 +28,10 @@ LEAD_W = 5
 LEAD_H = 5
 LEAD_U = 4
 LEAD_C = 1
+CAST_SPLIT_FROM = 0
+V_ODD_FROM = 0
 LEAD_L = 2
-V_FROM = 22
+V_FROM = 24
 BF16_FROM = -3
 LOAD_W = 4
 LOAD_H = 2
@@ -41,7 +43,7 @@ ACC_BUFS = 2
 LP_BUFS = 2
 VC_FROM = 1
 LOADS_FIRST_FROM = 0
-VC_TO = 12
+VC_TO = 5
 TILE_ORDER = (0, 4, 1, 5, 2, 6, 3, 7)
 
 FLOPS = 2 * 1024 * ODIM * KDIM + 2 * 1024 * ODIM * RANK
@@ -117,7 +119,7 @@ def tile_loratacmlp4_pb_kernel(tc, h, z, u, b, W_out_bytes, W_out_scale, b_out, 
         rows = sb.tile([P, 2, ODIM], BF16, name="rows", tag="rows")
         nc.vector.memset(rows[:].rearrange("p b n -> p (b n)").bitcast(F32), 0.0)
 
-        bias = sb.tile([P, 2, 2, CHUNK], F32, name="bias", tag="bias")
+        bias = sb.tile([P, N_CHUNKS, 2, CHUNK], F32, name="bias", tag="bias")
         zT = sb.tile([P, TOK_TILES, P], BF16, name="zT", tag="zT")
         brow = {}
 
@@ -130,13 +132,13 @@ def tile_loratacmlp4_pb_kernel(tc, h, z, u, b, W_out_bytes, W_out_scale, b_out, 
 
         def make_bias(j):
             for bb in range(2):
-                nc.gpsimd.tensor_tensor(out=bias[:, j - 2, bb, :], in0=brow[j][:, 1 + bb, :], in1=brow[j][:, 0, :], op=ALU.add)
+                nc.gpsimd.tensor_tensor(out=bias[:, j, bb, :], in0=brow[j][:, 1 + bb, :], in1=brow[j][:, 0, :], op=ALU.add)
 
         def v_cast(ot, part):
             return ot == 0 or VC_FROM <= ot < VC_TO and part == 1
 
         def v_lora(s):
-            return s >= V_FROM
+            return s >= V_FROM or s >= V_ODD_FROM and s % 2 == 1
 
         def w_cast(t, a):
             pair, gp = divmod(t, 2)
@@ -255,7 +257,7 @@ def tile_loratacmlp4_pb_kernel(tc, h, z, u, b, W_out_bytes, W_out_scale, b_out, 
                     out=lsum[s][:],
                     in0=lora_ps[s][:],
                     scalar=1.0 / RANK,
-                    in1=bias[:, j - 2, i // 4, :],
+                    in1=bias[:, j, i // 4, :],
                     op0=ALU.mult,
                     op1=ALU.add,
                 )
@@ -325,7 +327,7 @@ def tile_loratacmlp4_pb_kernel(tc, h, z, u, b, W_out_bytes, W_out_scale, b_out, 
                 for bb in range(2):
                     nc.sync.dma_start(out=rows[0:1, bb, :], in_=b_out.rearrange("(o n) -> o n", o=1))
                 nc.sync.dma_start(out=rows[1:2, :, :], in_=b.rearrange("b x y n -> (x y) b n"))
-            for j in (2, 3):
+            for j in range(min(V_FROM, V_ODD_FROM) // TOK_TILES, N_CHUNKS):
                 if q == 4 * j - LOAD_B:
                     load_bias(j)
                 if q == 4 * j - MAKE_B:
@@ -354,6 +356,8 @@ def tile_loratacmlp4_pb_kernel(tc, h, z, u, b, W_out_bytes, W_out_scale, b_out, 
                     main_half(2 * q + 1, 1)
             if 0 <= ot + LEAD_C < N_OT:
                 w_cast(ot + LEAD_C, 0)
+                if q < CAST_SPLIT_FROM:
+                    w_cast(ot + LEAD_C, 1)
             if q >= 0:
                 finish(2 * q)
                 if 2 * q + 1 < STEPS - 1:
@@ -383,9 +387,7 @@ def tile_loratacmlp4_pb_kernel(tc, h, z, u, b, W_out_bytes, W_out_scale, b_out, 
                 u_transpose(s)
             if in_steps(2 * (q + LEAD_L) + 1):
                 lora_matmul(2 * (q + LEAD_L) + 1)
-            if 0 <= ot + LEAD_C < N_OT:
+            if 0 <= ot + LEAD_C < N_OT and q >= CAST_SPLIT_FROM:
                 w_cast(ot + LEAD_C, 1)
-            if q < LOADS_FIRST_FROM - 1:
-                loads(q, ot)
-            if q == LOADS_FIRST_FROM - 1:
+            if q < LOADS_FIRST_FROM:
                 loads(q, ot)

@@ -36,8 +36,7 @@ BF16_FROM = -3
 LOAD_W = 4
 LOAD_H = 2
 LOAD_U = 2
-LOAD_B = 6
-MAKE_B = 3
+BIAS_AHEAD = 2
 TR_BUFS = 4
 ACC_BUFS = 2
 LP_BUFS = 2
@@ -121,18 +120,16 @@ def tile_loratacmlp4_pb_kernel(tc, h, z, u, b, W_out_bytes, W_out_scale, b_out, 
 
         bias = sb.tile([P, N_CHUNKS, 2, CHUNK], F32, name="bias", tag="bias")
         zT = sb.tile([P, TOK_TILES, P], BF16, name="zT", tag="zT")
-        brow = {}
 
-        def load_bias(j):
+        def bias_slice(bb, j):
             cols = slice(CHUNK * j, CHUNK * (j + 1))
-            brow[j] = sb.tile([P, 3, CHUNK], BF16, name="brow%d" % j, tag="brow", bufs=2)
-            nc.sync.dma_start(out=brow[j][:, 0, :], in_=b_out[cols].partition_broadcast(P))
-            for bb in range(2):
-                nc.sync.dma_start(out=brow[j][:, 1 + bb, :], in_=b_v[bb, cols].partition_broadcast(P))
+            bank = ps.tile([P, CHUNK], F32, name="bps%d_%d" % (bb, j), tag="tr", bufs=TR_BUFS)
+            nc.tensor.matmul(bank[:], lhsT=ones[:], rhs=rows[:, bb, cols], start=True, stop=True)
+            nc.scalar.activation(out=bias[:, j, bb, :], in_=bank[:], func=ACT.Copy, scale=1.0 / RANK)
 
-        def make_bias(j):
-            for bb in range(2):
-                nc.gpsimd.tensor_tensor(out=bias[:, j, bb, :], in0=brow[j][:, 1 + bb, :], in1=brow[j][:, 0, :], op=ALU.add)
+        def bias_batches(j):
+            steps = [s for s in range(TOK_TILES * j, TOK_TILES * (j + 1)) if v_lora(s)]
+            return sorted({TILE_ORDER[s % TOK_TILES] // 4 for s in steps})
 
         def v_cast(ot, part):
             return ot == 0 or VC_FROM <= ot < VC_TO and part == 1
@@ -327,11 +324,6 @@ def tile_loratacmlp4_pb_kernel(tc, h, z, u, b, W_out_bytes, W_out_scale, b_out, 
                 for bb in range(2):
                     nc.sync.dma_start(out=rows[0:1, bb, :], in_=b_out.rearrange("(o n) -> o n", o=1))
                 nc.sync.dma_start(out=rows[1:2, :, :], in_=b.rearrange("b x y n -> (x y) b n"))
-            for j in range(min(V_FROM, V_ODD_FROM) // TOK_TILES, N_CHUNKS):
-                if q == 4 * j - LOAD_B:
-                    load_bias(j)
-                if q == 4 * j - MAKE_B:
-                    make_bias(j)
             for s in range(STEPS):
                 if max(s // 2 - LEAD_U, BF16_FROM) - LOAD_U == q:
                     load_u(s)
@@ -365,6 +357,10 @@ def tile_loratacmlp4_pb_kernel(tc, h, z, u, b, W_out_bytes, W_out_scale, b_out, 
                 else:
                     finish_half(2 * q + 1, 0)
                     finish_half(2 * q + 1, 1)
+            for j in range(N_CHUNKS):
+                for n, bb in enumerate(reversed(bias_batches(j))):
+                    if q == 4 * j - BIAS_AHEAD - n:
+                        bias_slice(bb, j)
             if in_steps(2 * (q + LEAD_L)):
                 lora_matmul(2 * (q + LEAD_L))
             if 1 <= ot < N_OT + 1:

@@ -30,13 +30,15 @@ LEAD_U = 4
 LEAD_C = 1
 CAST_SPLIT_FROM = 0
 V_ODD_FROM = 0
+SWAP = 0
+SPLIT0 = 1
 LEAD_L = 2
-V_FROM = 24
+V_FROM = 26
 BF16_FROM = -3
 LOAD_W = 4
 LOAD_H = 2
 LOAD_U = 2
-BIAS_AHEAD = 2
+BIAS_AHEAD = 3
 TR_BUFS = 4
 ACC_BUFS = 2
 LP_BUFS = 2
@@ -84,6 +86,10 @@ def tile_loratacmlp4_pb_kernel(tc, h, z, u, b, W_out_bytes, W_out_scale, b_out, 
                 wbytes[j] = sb.tile([P, 4, KDIM], U8, name="wbytes%d" % j, tag="wbytes", bufs=3)
             if ot < 2:
                 cols = slice(KDIM // 2 * ot, KDIM // 2 * (ot + 1))
+                if SPLIT0 and ot == 0:
+                    for lo in range(2):
+                        nc.sync.dma_start(out=wbytes[0][:, lo, cols], in_=w_v[0][:, lo, cols])
+                    return
                 nc.sync.dma_start(out=wbytes[0][:, 0:2, cols], in_=w_v[0][:, 0:2, cols])
                 return
             nc.sync.dma_start(out=wbytes[j][:, a, :], in_=w_v[j][:, a, :])
@@ -328,6 +334,12 @@ def tile_loratacmlp4_pb_kernel(tc, h, z, u, b, W_out_bytes, W_out_scale, b_out, 
                 if max(s // 2 - LEAD_U, BF16_FROM) - LOAD_U == q:
                     load_u(s)
 
+        def ahead(q):
+            return 2 * (q + LEAD_L) + 1 - SWAP
+
+        def behind(q):
+            return 2 * (q + LEAD_L) + SWAP
+
         for q in range(FIRST_ROUND, 16):
             ot = q + LEAD_W
             if q >= LOADS_FIRST_FROM:
@@ -337,8 +349,8 @@ def tile_loratacmlp4_pb_kernel(tc, h, z, u, b, W_out_bytes, W_out_scale, b_out, 
             if 0 <= ot - 1 < N_OT:
                 w_scale(ot - 1, 0)
                 w_scale(ot - 1, 1)
-            if in_steps(2 * (q - 1 + LEAD_L) + 1):
-                lora_out(2 * (q - 1 + LEAD_L) + 1)
+            if in_steps(behind(q - 1)):
+                lora_out(behind(q - 1))
             if q >= 0:
                 main_matmul(2 * q)
                 if 2 * q + 1 < STEPS - 1:
@@ -359,18 +371,18 @@ def tile_loratacmlp4_pb_kernel(tc, h, z, u, b, W_out_bytes, W_out_scale, b_out, 
                     finish_half(2 * q + 1, 1)
             for j in range(N_CHUNKS):
                 for n, bb in enumerate(reversed(bias_batches(j))):
-                    if q == 4 * j - BIAS_AHEAD - n:
+                    if q == 4 * j - (BIAS_AHEAD if j else 2) - n:
                         bias_slice(bb, j)
-            if in_steps(2 * (q + LEAD_L)):
-                lora_matmul(2 * (q + LEAD_L))
+            if in_steps(ahead(q)):
+                lora_matmul(ahead(q))
             if 1 <= ot < N_OT + 1:
                 for gg in range(2):
                     w_quantize((ot - 1) // 2, 2 * ((ot - 1) % 2) + gg)
             for n in (2 * (q + LEAD_H - 1), 2 * (q + LEAD_H - 1) + 1):
                 if 0 <= n < TOK_TILES:
                     h_quantize(TILE_ORDER[n])
-            if in_steps(2 * (q + LEAD_L)):
-                lora_out(2 * (q + LEAD_L))
+            if in_steps(ahead(q)):
+                lora_out(ahead(q))
             if 0 <= ot < N_OT:
                 w_transpose(ot, 0)
                 w_transpose(ot, 1)
@@ -381,8 +393,8 @@ def tile_loratacmlp4_pb_kernel(tc, h, z, u, b, W_out_bytes, W_out_scale, b_out, 
                 z_prep()
             for s in u_round(q):
                 u_transpose(s)
-            if in_steps(2 * (q + LEAD_L) + 1):
-                lora_matmul(2 * (q + LEAD_L) + 1)
+            if in_steps(behind(q)):
+                lora_matmul(behind(q))
             if 0 <= ot + LEAD_C < N_OT and q >= CAST_SPLIT_FROM:
                 w_cast(ot + LEAD_C, 1)
             if q < LOADS_FIRST_FROM:

from contextlib import ExitStack

import concourse.mybir as mybir
from concourse.masks import make_identity

F32 = mybir.dt.float32
BF16 = mybir.dt.bfloat16
U32 = mybir.dt.uint32
U8 = mybir.dt.uint8
FP8 = mybir.dt.float8_e4m3fn
FP8X4 = mybir.dt.float8_e4m3fn_x4
ALU = mybir.AluOpType
ACT = mybir.ActivationFunctionType

P = 128
TOK_TILES = 8
KDIM = 2048
ODIM = 2048
RANK = 128
PASSES = 4
CHUNK = 512
HALF = 256
N_CHUNKS = 4
N_OT = 16
STEPS = 32
FIRST_ROUND = -9
LEAD_W = 5
LEAD_H = 5
LEAD_U = 4
LEAD_C = 1
CAST_SPLIT_FROM = 0
V_ODD_FROM = 0
SWAP = 0
SPLIT0 = 1
LEAD_L = 2
V_FROM = 26
BF16_FROM = -3
LOAD_W = 4
LOAD_H = 2
LOAD_U = 2
BIAS_AHEAD = 3
TR_BUFS = 4
ACC_BUFS = 2
LP_BUFS = 2
VC_FROM = 1
LOADS_FIRST_FROM = 0
VC_TO = 5
TILE_ORDER = (0, 4, 1, 5, 2, 6, 3, 7)

FLOPS = 2 * 1024 * ODIM * KDIM + 2 * 1024 * ODIM * RANK


def tile_loratacmlp4_pb_kernel(tc, h, z, u, b, W_out_bytes, W_out_scale, b_out, out):
    nc = tc.nc
    with ExitStack() as ctx:
        sb = ctx.enter_context(tc.tile_pool(name="sb", bufs=1))
        ps = ctx.enter_context(tc.psum_pool(name="ps", bufs=2))
        ctx.enter_context(tc.manual_schedule())

        h_v = h.rearrange("b k f c -> (b k) f c")
        out_v = out.rearrange("b k f n -> (b k) f n")
        w_v = W_out_bytes.rearrange("(c a p) k -> c p a k", a=4, p=P)
        u_v = u.rearrange("b k (c a p) r -> (b k) c p a r", c=N_CHUNKS, a=4, p=P)
        b_v = b.rearrange("b x y n -> (b x y) n")

        wbytes = {}
        wcast = {}
        wgrp = {}
        wcodes = {}
        wscales = {}
        hraw = {}
        hgrp = {}
        hcodes = {}
        hscales = {}
        uraw = {}
        uT = {}
        lora_ps = {}
        acc_ps = {}
        lsum = {}
        acc_half = {}
        banks = {}

        def load_w(ot):
            j, a = divmod(ot, 4)
            if j not in wbytes:
                wbytes[j] = sb.tile([P, 4, KDIM], U8, name="wbytes%d" % j, tag="wbytes", bufs=3)
            if ot < 2:
                cols = slice(KDIM // 2 * ot, KDIM // 2 * (ot + 1))
                if SPLIT0 and ot == 0:
                    for lo in range(2):
                        nc.sync.dma_start(out=wbytes[0][:, lo, cols], in_=w_v[0][:, lo, cols])
                    return
                nc.sync.dma_start(out=wbytes[0][:, 0:2, cols], in_=w_v[0][:, 0:2, cols])
                return
            nc.sync.dma_start(out=wbytes[j][:, a, :], in_=w_v[j][:, a, :])

        def load_h(i):
            hraw[i] = sb.tile([P, KDIM], BF16, name="hraw%d" % i, tag="hraw", bufs=4)
            nc.sync.dma_start(out=hraw[i][:], in_=h_v[i])

        def load_u(s):
            j, m = s // TOK_TILES, TILE_ORDER[s % TOK_TILES]
            uraw[s] = sb.tile([P, 4, RANK], BF16, name="uraw%d" % s, tag="uraw", bufs=8)
            nc.sync.dma_start(out=uraw[s][:], in_=u_v[m][j])

        zraw = sb.tile([P, TOK_TILES, RANK], BF16, name="zraw", tag="zraw")
        sc_col = sb.tile([P, KDIM // P], F32, name="sc_col", tag="sc_col")
        nc.scalar.dma_start(
            out=sc_col[:].rearrange("p (g c) -> p g c", c=4),
            in_=W_out_scale.rearrange("o (g p c) -> p (o g) c", g=PASSES, p=P, c=4),
        )

        warm = sb.tile([P, 2], F32, name="warm", tag="warm")
        nc.vector.memset(warm[:], 0.0)
        nc.scalar.activation(out=warm[:, 1:2], in_=warm[:, 0:1], func=ACT.Gelu)

        ident_f = sb.tile([P, P], F32, name="ident_f", tag="ident_f")
        make_identity(nc, ident_f[:])
        ident_b = sb.tile([P, P], BF16, name="ident_b", tag="ident_b")
        make_identity(nc, ident_b[:])

        ones = sb.tile([P, P], BF16, name="ones", tag="ones")
        nc.vector.memset(ones[:], float(RANK))
        rows = sb.tile([P, 2, ODIM], BF16, name="rows", tag="rows")
        nc.vector.memset(rows[:].rearrange("p b n -> p (b n)").bitcast(F32), 0.0)

        bias = sb.tile([P, N_CHUNKS, 2, CHUNK], F32, name="bias", tag="bias")
        zT = sb.tile([P, TOK_TILES, P], BF16, name="zT", tag="zT")

        def bias_slice(bb, j):
            cols = slice(CHUNK * j, CHUNK * (j + 1))
            bank = ps.tile([P, CHUNK], F32, name="bps%d_%d" % (bb, j), tag="tr", bufs=TR_BUFS)
            nc.tensor.matmul(bank[:], lhsT=ones[:], rhs=rows[:, bb, cols], start=True, stop=True)
            nc.scalar.activation(out=bias[:, j, bb, :], in_=bank[:], func=ACT.Copy, scale=1.0 / RANK)

        def bias_batches(j):
            steps = [s for s in range(TOK_TILES * j, TOK_TILES * (j + 1)) if v_lora(s)]
            return sorted({TILE_ORDER[s % TOK_TILES] // 4 for s in steps})

        def v_cast(ot, part):
            return ot == 0 or VC_FROM <= ot < VC_TO and part == 1

        def v_lora(s):
            return s >= V_FROM or s >= V_ODD_FROM and s % 2 == 1

        def w_cast(t, a):
            pair, gp = divmod(t, 2)
            j, lo = divmod(2 * pair + a, 4)
            if a == 0:
                wcast[t] = sb.tile([P, 2, KDIM // 2], BF16, name="wcast%d" % t, tag="wcast", bufs=3)
            pieces = 2 if t == 0 else 1
            width = KDIM // 2 // pieces
            for c in range(pieces):
                dst = wcast[t][:, a, width * c : width * (c + 1)]
                src = wbytes[j][:, lo, KDIM // 2 * gp + width * c : KDIM // 2 * gp + width * (c + 1)].bitcast(FP8)
                if v_cast(t, a):
                    nc.vector.tensor_copy(out=dst, in_=src)
                else:
                    nc.scalar.copy(out=dst, in_=src)

        def w_transpose(t, gg):
            words = wcast[t][:].rearrange("p a k -> p (a k)").bitcast(F32)
            bank = ps.tile([P, 2, 256], F32, name="wtr%d_%d" % (t, gg), tag="tr", bufs=TR_BUFS)
            for a in range(2):
                for w in range(2):
                    first = 512 * a + 256 * gg + w
                    nc.tensor.transpose(bank[:, w, P * a : P * (a + 1)], words[:, first : first - w + 256 : 2], ident_f[:])
            banks[t, gg] = bank

        def w_scale(t, gg):
            pair, gp = divmod(t, 2)
            g = 2 * gp + gg
            if pair not in wgrp:
                wgrp[pair] = sb.tile(
                    [P, PASSES, 256, 4], BF16, name="wgrp%d" % pair, tag="wgrp", bufs=3, align_bytes=64
                )
            nc.vector.tensor_tensor(
                out=wgrp[pair][:, g, :, :].rearrange("p o (w e) -> p o w e", e=2),
                in0=banks[t, gg][:].bitcast(BF16).rearrange("p w (o e) -> p o w e", e=2),
                in1=sc_col[:, 4 * g : 4 * g + 4].rearrange("p (w e) -> p w e", e=2).unsqueeze(1).to_broadcast([P, 256, 2, 2]),
                op=ALU.mult,
            )

        def w_quantize(pair, g):
            j, half = divmod(pair, 2)
            if j not in wcodes:
                wcodes[j] = sb.tile([P, PASSES, CHUNK], U32, name="wcodes%d" % j, tag="wcodes", bufs=2, align_bytes=64)
                wscales[j] = sb.tile([P, PASSES, CHUNK], U8, name="wscales%d" % j, tag="wscales", bufs=2, align_bytes=64)
            cols = slice(256 * half, 256 * half + 256)
            nc.vector.quantize_mx(
                out=wcodes[j][:, g, cols].bitcast(FP8X4),
                scales=wscales[j][:, g, cols],
                in_=wgrp[pair][:, g, :, :].rearrange("p o t -> p (o t)"),
            )

        def h_transpose(i):
            hgrp[i] = sb.tile([P, PASSES, P, 4], BF16, name="hgrp%d" % i, tag="hgrp", bufs=4, align_bytes=64)
            words = hraw[i][:].bitcast(F32)
            for gp in range(2):
                bank = ps.tile([P, 2, 2, P], F32, name="htr%d_%d" % (i, gp), tag=("acc", "lp")[gp], bufs=2)
                for gg in range(2):
                    g = 2 * gp + gg
                    for w in range(2):
                        nc.tensor.transpose(bank[:, gg, w, :], words[:, 256 * g + w : 256 * (g + 1) : 2], ident_f[:])
                nc.scalar.copy(
                    out=hgrp[i][:].bitcast(F32)[:, 2 * gp : 2 * gp + 2, :, :],
                    in_=bank[:].rearrange("p g w r -> p g r w"),
                )

        def h_quantize(i):
            hcodes[i] = sb.tile([P, PASSES, P], U32, name="hcodes%d" % i, tag="hcodes%d" % i, align_bytes=64)
            hscales[i] = sb.tile([P, PASSES, P], U8, name="hscales%d" % i, tag="hscales%d" % i, align_bytes=64)
            nc.vector.quantize_mx(
                out=hcodes[i][:].rearrange("p g r -> p (g r)").bitcast(FP8X4),
                scales=hscales[i][:].rearrange("p g r -> p (g r)"),
                in_=hgrp[i][:].rearrange("p g r t -> p (g r t)"),
            )

        def z_prep():
            for half in range(2):
                bank = ps.tile([P, 4, P], BF16, name="ztr%d" % half, tag="acc", bufs=2)
                for m in range(4):
                    nc.tensor.transpose(bank[:, m, :], zraw[:, 4 * half + m, :], ident_b[:])
                nc.scalar.copy(
                    out=zT[:, 4 * half : 4 * half + 4, :].rearrange("p m q -> p (m q)").bitcast(F32),
                    in_=bank[:].rearrange("p m q -> p (m q)").bitcast(F32),
                )

        def u_transpose(s):
            j, n = divmod(s, TOK_TILES)
            if j not in uT:
                uT[j] = sb.tile([P, TOK_TILES, CHUNK], BF16, name="uT%d" % j, tag="uT", bufs=2)
            bank = ps.tile([P, 2, 4, P], BF16, name="utr%d" % s, tag="tr", bufs=TR_BUFS)
            for e in range(2):
                for a in range(4):
                    nc.tensor.transpose(bank[:, e, a, :], uraw[s + e][:, a, :], ident_b[:])
            banks["u", s] = bank

        def u_copy(s):
            j, n = divmod(s, TOK_TILES)
            nc.scalar.copy(
                out=uT[j][:, n : n + 2, :].rearrange("p e c -> p (e c)").bitcast(F32),
                in_=banks["u", s][:].rearrange("p e a q -> p (e a q)").bitcast(F32),
            )

        def lora_matmul(s):
            j, i = s // TOK_TILES, TILE_ORDER[s % TOK_TILES]
            lora_ps[s] = ps.tile([P, CHUNK], F32, name="lp%d" % s, tag="lp", bufs=LP_BUFS)
            nc.tensor.matmul(lora_ps[s][:], lhsT=zT[:, i, :], rhs=uT[j][:, s % TOK_TILES, :], start=True, stop=v_lora(s))
            if not v_lora(s):
                nc.tensor.matmul(
                    lora_ps[s][:], lhsT=ones[:], rhs=rows[:, i // 4, CHUNK * j : CHUNK * (j + 1)], start=False, stop=True
                )

        def lora_out(s):
            j, i = s // TOK_TILES, TILE_ORDER[s % TOK_TILES]
            lsum[s] = sb.tile([P, CHUNK], F32, name="lsum%d" % s, tag="lsum", bufs=6)
            if v_lora(s):
                nc.vector.scalar_tensor_tensor(
                    out=lsum[s][:],
                    in0=lora_ps[s][:],
                    scalar=1.0 / RANK,
                    in1=bias[:, j, i // 4, :],
                    op0=ALU.mult,
                    op1=ALU.add,
                )
                return
            nc.scalar.activation(out=lsum[s][:], in_=lora_ps[s][:], func=ACT.Copy, scale=1.0 / RANK)

        def main_matmul(s):
            j, i = s // TOK_TILES, TILE_ORDER[s % TOK_TILES]
            acc_ps[s] = ps.tile([P, CHUNK], F32, name="acc%d" % s, tag="acc", bufs=ACC_BUFS)
            for g in range(PASSES):
                nc.tensor.matmul_mx(
                    out=acc_ps[s][:],
                    lhsT=hcodes[i][:, g, :].bitcast(FP8X4),
                    lhsT_scale=hscales[i][:, g, :],
                    rhs=wcodes[j][:, g, :].bitcast(FP8X4),
                    rhs_scale=wscales[j][:, g, :],
                    start=(g == 0),
                    stop=(g == PASSES - 1),
                )

        def finish(s):
            j, i = s // TOK_TILES, TILE_ORDER[s % TOK_TILES]
            total = sb.tile([P, CHUNK], F32, name="total%d" % s, tag="total", bufs=3)
            nc.vector.tensor_tensor(out=total[:], in0=acc_ps[s][:], in1=lsum[s][:], op=ALU.add)
            res = sb.tile([P, CHUNK], F32, name="res%d" % s, tag="res", bufs=4)
            nc.scalar.activation(out=res[:], in_=total[:], func=ACT.Gelu)
            nc.sync.dma_start(out=out_v[i][:, CHUNK * j : CHUNK * (j + 1)], in_=res[:])

        def main_half(s, part):
            j, i = s // TOK_TILES, TILE_ORDER[s % TOK_TILES]
            cols = slice(HALF * part, HALF * (part + 1))
            acc_half[part] = ps.tile([P, HALF], F32, name="acch%d" % part, tag="acc" if part == 0 else "lp", bufs=2)
            for g in range(PASSES):
                nc.tensor.matmul_mx(
                    out=acc_half[part][:],
                    lhsT=hcodes[i][:, g, :].bitcast(FP8X4),
                    lhsT_scale=hscales[i][:, g, :],
                    rhs=wcodes[j][:, g, cols].bitcast(FP8X4),
                    rhs_scale=wscales[j][:, g, cols],
                    start=(g == 0),
                    stop=(g == PASSES - 1),
                )

        def finish_half(s, part):
            j, i = s // TOK_TILES, TILE_ORDER[s % TOK_TILES]
            cols = slice(HALF * part, HALF * (part + 1))
            total = sb.tile([P, HALF], F32, name="totalh%d" % part, tag="total", bufs=3)
            nc.vector.tensor_tensor(out=total[:], in0=acc_half[part][:], in1=lsum[s][:, cols], op=ALU.add)
            res = sb.tile([P, HALF], F32, name="resh%d" % part, tag="res", bufs=4)
            nc.scalar.activation(out=res[:], in_=total[:], func=ACT.Gelu)
            nc.sync.dma_start(out=out_v[i][:, CHUNK * j + HALF * part : CHUNK * j + HALF * (part + 1)], in_=res[:])

        def in_steps(s):
            return 0 <= s < STEPS

        def u_round(q):
            return [s for s in range(0, STEPS, 2) if max(s // 2 - LEAD_U, BF16_FROM) == q]

        def loads(q, ot):
            if 0 <= ot + LOAD_W < N_OT:
                load_w(ot + LOAD_W)
            for n in (2 * (q + LEAD_H + LOAD_H), 2 * (q + LEAD_H + LOAD_H) + 1):
                if 0 <= n < TOK_TILES:
                    load_h(TILE_ORDER[n])
            if q == BF16_FROM - LOAD_U:
                nc.sync.dma_start(out=zraw[:], in_=z.rearrange("b k f r -> f (b k) r"))
                for bb in range(2):
                    nc.sync.dma_start(out=rows[0:1, bb, :], in_=b_out.rearrange("(o n) -> o n", o=1))
                nc.sync.dma_start(out=rows[1:2, :, :], in_=b.rearrange("b x y n -> (x y) b n"))
            for s in range(STEPS):
                if max(s // 2 - LEAD_U, BF16_FROM) - LOAD_U == q:
                    load_u(s)

        def ahead(q):
            return 2 * (q + LEAD_L) + 1 - SWAP

        def behind(q):
            return 2 * (q + LEAD_L) + SWAP

        for q in range(FIRST_ROUND, 16):
            ot = q + LEAD_W
            if q >= LOADS_FIRST_FROM:
                loads(q, ot)
            for s in u_round(q - 1):
                u_copy(s)
            if 0 <= ot - 1 < N_OT:
                w_scale(ot - 1, 0)
                w_scale(ot - 1, 1)
            if in_steps(behind(q - 1)):
                lora_out(behind(q - 1))
            if q >= 0:
                main_matmul(2 * q)
                if 2 * q + 1 < STEPS - 1:
                    main_matmul(2 * q + 1)
                else:
                    main_half(2 * q + 1, 0)
                    main_half(2 * q + 1, 1)
            if 0 <= ot + LEAD_C < N_OT:
                w_cast(ot + LEAD_C, 0)
                if q < CAST_SPLIT_FROM:
                    w_cast(ot + LEAD_C, 1)
            if q >= 0:
                finish(2 * q)
                if 2 * q + 1 < STEPS - 1:
                    finish(2 * q + 1)
                else:
                    finish_half(2 * q + 1, 0)
                    finish_half(2 * q + 1, 1)
            for j in range(N_CHUNKS):
                for n, bb in enumerate(reversed(bias_batches(j))):
                    if q == 4 * j - (BIAS_AHEAD if j else 2) - n:
                        bias_slice(bb, j)
            if in_steps(ahead(q)):
                lora_matmul(ahead(q))
            if 1 <= ot < N_OT + 1:
                for gg in range(2):
                    w_quantize((ot - 1) // 2, 2 * ((ot - 1) % 2) + gg)
            for n in (2 * (q + LEAD_H - 1), 2 * (q + LEAD_H - 1) + 1):
                if 0 <= n < TOK_TILES:
                    h_quantize(TILE_ORDER[n])
            if in_steps(ahead(q)):
                lora_out(ahead(q))
            if 0 <= ot < N_OT:
                w_transpose(ot, 0)
                w_transpose(ot, 1)
            for n in (2 * (q + LEAD_H), 2 * (q + LEAD_H) + 1):
                if 0 <= n < TOK_TILES:
                    h_transpose(TILE_ORDER[n])
            if q == BF16_FROM:
                z_prep()
            for s in u_round(q):
                u_transpose(s)
            if in_steps(behind(q)):
                lora_matmul(behind(q))
            if 0 <= ot + LEAD_C < N_OT and q >= CAST_SPLIT_FROM:
                w_cast(ot + LEAD_C, 1)
            if q < LOADS_FIRST_FROM:
                loads(q, ot)
